import numpy as np
import ml_dtypes


def mxq(x, axis, fmt="e4m3"):
    dtype, down = {"e4m3": (ml_dtypes.float8_e4m3fn, 7), "e5m2": (ml_dtypes.float8_e5m2, 14)}[fmt]
    v = np.moveaxis(np.asarray(x, np.float32).astype(ml_dtypes.bfloat16).astype(np.float64), axis, -1)
    blocks = v.reshape(v.shape[:-1] + (-1, 32))
    amax = np.abs(blocks).max(-1, keepdims=True)
    byte = np.maximum(np.where(amax > 0, np.frexp(amax)[1] - 1 + 127, 0) - down, 1)
    scale = np.exp2(byte - 127.0)
    codes = (blocks / scale).astype(np.float32).astype(dtype).astype(np.float64)
    return np.moveaxis((codes * scale).reshape(v.shape), -1, axis)


WIDE = False


def mx_kscale(k):
    if not WIDE:
        return np.ones(k)
    levels = np.array([10, -10, 5, -5, 0])
    a = np.random.permutation(np.resize(levels, k // 512 * 4)).reshape(k // 512, 4)
    idx = np.arange(k)
    return np.exp2(a[idx // 512, idx % 128 // 32])


BF16 = ml_dtypes.bfloat16


def bf(x):
    return np.asarray(x, np.float32).astype(BF16)


def f64(x):
    return np.asarray(x).astype(np.float64)


B, N, C, DIM, H = 2, 64, 1024, 1024, 16
D = DIM // H // 2
LAYER_NUM = 12
LAM_INIT = 0.8 - 0.6 * np.exp(-0.3 * LAYER_NUM)
SCALE = D ** -0.5


def split_qk(y):
    y = y.reshape(B, N, H, D, 2)
    return np.moveaxis(y, -1, 2).reshape(B, N, 2 * H, D)


def setup_inputs():
    s = mx_kscale(C)
    ls = 0.45 / D ** 0.25
    return {"x": bf(np.random.standard_normal((B, N, C)) * s),
            "Wq": bf(np.random.standard_normal((DIM, C)) / np.sqrt(C) / s),
            "Wk": bf(np.random.standard_normal((DIM, C)) / np.sqrt(C) / s),
            "lq1": bf(np.random.standard_normal(D) * ls),
            "lq2": bf(np.random.standard_normal(D) * ls),
            "lk1": bf(np.random.standard_normal(D) * ls),
            "lk2": bf(np.random.standard_normal(D) * ls)}


def reference(x, Wq, Wk, lq1, lq2, lk1, lk2):
    xq = mxq(f64(x), 2, "e4m3")
    q = split_qk(xq @ mxq(f64(Wq), 1, "e4m3").T) * SCALE
    k = split_qk(xq @ mxq(f64(Wk), 1, "e4m3").T)
    sc = np.stack([(q[:, :, i:i + 1, :] * k).sum(-1) for i in range(2 * H)], axis=2)
    e = np.exp(sc - sc.max(-1, keepdims=True))
    att = e / e.sum(-1, keepdims=True)
    lam = np.exp(np.sum(f64(lq1) * f64(lk1))) - np.exp(np.sum(f64(lq2) * f64(lk2))) + LAM_INIT
    return att[:, :, :H, :H] - lam * att[:, :, H:, H:]

@@ -1,0 +1,230 @@
+from contextlib import ExitStack
+import math
+
+import concourse.mybir as mybir
+from concourse.masks import make_identity
+
+F32 = mybir.dt.float32
+BF16 = mybir.dt.bfloat16
+U32 = mybir.dt.uint32
+U8 = mybir.dt.uint8
+FP8X4 = mybir.dt.float8_e4m3fn_x4
+ALU = mybir.AluOpType
+ACT = mybir.ActivationFunctionType
+AXIS = mybir.AxisListType
+
+P = 128
+K = 1024
+K_PASS = 512
+PASSES = K // K_PASS
+WORDS = K // 2
+HEADS = 16
+ROWS = 2 * HEADS
+D = 32
+QUAD = 32
+QUADS = P // QUAD
+W_TILES = 4
+HALF = ROWS // 2
+Y_HALF = HEADS * D
+SCALE = D ** -0.5
+LAM_INIT = 0.8 - 0.6 * math.exp(-0.3 * 12)
+
+FLOPS = 2 * P * K * 2 * K + 2 * P * ROWS * ROWS * D
+
+
+def regroup_rows(nc, banks, ident, row_words, grouped_words):
+    bank = banks.tile([P, 2 * PASSES, P], F32, tag="bank", name="bank")
+    for chunk in range(2 * PASSES):
+        nc.tensor.transpose(bank[:, chunk, :], row_words[:, chunk * P : (chunk + 1) * P], ident)
+    nc.scalar.copy(
+        out=grouped_words.rearrange("p (g r u) -> p g r u", g=PASSES, u=2),
+        in_=bank[:].rearrange("p (g u) r -> p g r u", u=2),
+    )
+
+
+def project(nc, stage, banks, ident, x_codes, x_scales, w_tiles, y_halves):
+    for s in range(W_TILES):
+        w_words = w_tiles[s][:].bitcast(F32)
+        grouped = stage.tile([P, 2 * PASSES * P * 4], BF16, align_bytes=64, name="grouped")
+        grouped_words = grouped[:].bitcast(F32)
+        for j in range(2):
+            regroup_rows(
+                nc,
+                banks,
+                ident,
+                w_words[:, j * WORDS : (j + 1) * WORDS],
+                grouped_words[:, j * WORDS : (j + 1) * WORDS],
+            )
+        w_codes = stage.tile([P, 2 * PASSES * P], U32, align_bytes=64, name="w_codes")
+        w_scales = stage.tile([P, 2 * PASSES * P], U8, align_bytes=64, name="w_scales")
+        nc.vector.quantize_mx(out=w_codes[:].bitcast(FP8X4), scales=w_scales[:], in_=grouped[:])
+        for j in range(2):
+            for g in range(PASSES):
+                x_cols = slice(g * P, (g + 1) * P)
+                w_cols = slice((j * PASSES + g) * P, (j * PASSES + g + 1) * P)
+                nc.tensor.matmul_mx(
+                    out=y_halves[j][:, s * P : (s + 1) * P],
+                    lhsT=x_codes[:, x_cols].bitcast(FP8X4),
+                    lhsT_scale=x_scales[:, x_cols],
+                    rhs=w_codes[:, w_cols].bitcast(FP8X4),
+                    rhs_scale=w_scales[:, w_cols],
+                    start=(g == 0),
+                    stop=(g == PASSES - 1),
+                )
+
+
+def tile_differentialattention_pa_s_kernel(tc, x, Wq, Wk, lq1, lq2, lk1, lk2, out):
+    nc = tc.nc
+    with ExitStack() as ctx:
+        keep = ctx.enter_context(tc.tile_pool(name="keep", bufs=1))
+        stage = ctx.enter_context(tc.tile_pool(name="stage", bufs=3))
+        banks = ctx.enter_context(tc.psum_pool(name="banks", bufs=4))
+        y_pool = ctx.enter_context(tc.psum_pool(name="y_pool", bufs=1))
+
+        x_sb = keep.tile([P, K], BF16, name="x_sb")
+        nc.sync.dma_start(out=x_sb[:], in_=x.rearrange("b n k -> (b n) k"))
+        w_tiles = {}
+        for name, w in (("q", Wq), ("k", Wk)):
+            w_view = w.rearrange("(s p j) k -> s p (j k)", p=P, j=2)
+            w_tiles[name] = []
+            for s in range(W_TILES):
+                w_sb = keep.tile([P, 2 * K], BF16, name="w_%s%d" % (name, s))
+                nc.sync.dma_start(out=w_sb[:], in_=w_view[s])
+                w_tiles[name].append(w_sb)
+
+        lam_rows = keep.tile([P, 4 * D], BF16, name="lam_rows")
+        nc.vector.memset(lam_rows[:], 0.0)
+        for n, vector in enumerate((lq1, lq2, lk1, lk2)):
+            nc.scalar.dma_start(
+                out=lam_rows[0:1, n * D : (n + 1) * D], in_=vector.rearrange("(o d) -> o d", o=1)
+            )
+
+        ident = keep.tile([P, P], F32, name="ident")
+        make_identity(nc, ident[:])
+        ones = keep.tile([P, P], BF16, name="ones")
+        nc.vector.memset(ones[:], 1.0)
+        warm = keep.tile([P, 2], F32, name="warm")
+        nc.vector.memset(warm[:], 0.0)
+        nc.scalar.activation(out=warm[:, 1:2], in_=warm[:, 0:1], func=ACT.Exp)
+        q_blocks = keep.tile([P, QUAD, QUADS, ROWS], F32, name="q_blocks")
+        nc.vector.memset(q_blocks[:], 0.0)
+
+        x_grouped = keep.tile([P, PASSES * P * 4], BF16, align_bytes=64, name="x_grouped")
+        regroup_rows(nc, banks, ident[:], x_sb[:].bitcast(F32), x_grouped[:].bitcast(F32))
+        x_codes = keep.tile([P, PASSES * P], U32, align_bytes=64, name="x_codes")
+        x_scales = keep.tile([P, PASSES * P], U8, align_bytes=64, name="x_scales")
+        nc.vector.quantize_mx(out=x_codes[:].bitcast(FP8X4), scales=x_scales[:], in_=x_grouped[:])
+
+        lam_bank = banks.tile([P, 4 * D], F32, tag="bank", name="lam_bank")
+        nc.tensor.matmul(out=lam_bank[:], lhsT=ones[:], rhs=lam_rows[:], start=True, stop=True)
+        lam_all = keep.tile([P, 4 * D], F32, name="lam_all")
+        nc.scalar.copy(out=lam_all[:], in_=lam_bank[:])
+        lam_prod = keep.tile([P, 2, D], F32, name="lam_prod")
+        nc.vector.tensor_tensor(
+            out=lam_prod[:].rearrange("p n d -> p (n d)"),
+            in0=lam_all[:, 0 : 2 * D],
+            in1=lam_all[:, 2 * D : 4 * D],
+            op=ALU.mult,
+        )
+        lam_dots = keep.tile([P, 2], F32, name="lam_dots")
+        nc.vector.tensor_reduce(out=lam_dots[:], in_=lam_prod[:], axis=AXIS.X, op=ALU.add)
+        lam_exp = keep.tile([P, 2], F32, name="lam_exp")
+        nc.scalar.activation(out=lam_exp[:], in_=lam_dots[:], func=ACT.Exp)
+        neg_lam = keep.tile([P, 1], F32, name="neg_lam")
+        nc.vector.scalar_tensor_tensor(
+            out=neg_lam[:],
+            in0=lam_exp[:, 1:2],
+            scalar=-LAM_INIT,
+            in1=lam_exp[:, 0:1],
+            op0=ALU.add,
+            op1=ALU.subtract,
+        )
+
+        yq = [y_pool.tile([P, Y_HALF], F32, name="yq%d" % j) for j in range(2)]
+        project(nc, stage, banks, ident[:], x_codes, x_scales, w_tiles["q"], yq)
+        q_t = keep.tile([P, ROWS * QUAD], F32, align_bytes=64, name="q_t")
+        for j in range(2):
+            nc.vector.transpose(out=q_t[:, j * Y_HALF : (j + 1) * Y_HALF], in_=yq[j][:])
+        for c in range(QUADS):
+            rows = slice(c * QUAD, (c + 1) * QUAD)
+            source = q_t[rows, :].rearrange("p (i t) -> p t i", t=QUAD)
+            if c % 2 == 0:
+                nc.vector.tensor_copy(out=q_blocks[rows, :, c, :], in_=source)
+            else:
+                nc.gpsimd.tensor_scalar(
+                    out=q_blocks[rows, :, c, :],
+                    in0=source,
+                    scalar1=1.0,
+                    scalar2=0.0,
+                    op0=ALU.mult,
+                    op1=ALU.add,
+                )
+
+        yk = [y_pool.tile([P, Y_HALF], F32, name="yk%d" % j) for j in range(2)]
+        project(nc, stage, banks, ident[:], x_codes, x_scales, w_tiles["k"], yk)
+        k_t = keep.tile([P, ROWS * QUAD], F32, align_bytes=64, name="k_t")
+        for j in range(2):
+            nc.vector.transpose(out=k_t[:, j * Y_HALF : (j + 1) * Y_HALF], in_=yk[j][:])
+        k_cols = keep.tile([P, QUAD, ROWS], F32, name="k_cols")
+        k_t_view = k_t[:].rearrange("p (m t) -> p t m", t=QUAD)
+        nc.vector.tensor_copy(out=k_cols[:, 0:HALF, :], in_=k_t_view[:, 0:HALF, :])
+        nc.scalar.copy(out=k_cols[:, HALF:QUAD, :], in_=k_t_view[:, HALF:QUAD, :])
+
+        expd = keep.tile([P, ROWS, QUAD], F32, align_bytes=64, name="expd")
+        sums = keep.tile([P, QUAD], F32, align_bytes=64, name="sums")
+        for half in range(2):
+            ts = slice(half * HALF, (half + 1) * HALF)
+            scores = banks.tile([P, HALF, ROWS], F32, tag="bank", name="scores")
+            for t in range(HALF):
+                nc.tensor.matmul(
+                    out=scores[:, t, :],
+                    lhsT=q_blocks[:, half * HALF + t].rearrange("p c i -> p (c i)"),
+                    rhs=k_cols[:, half * HALF + t, :],
+                    start=True,
+                    stop=True,
+                )
+            top = keep.tile([P, HALF], F32, name="top%d" % half)
+            nc.vector.tensor_reduce(out=top[:], in_=scores[:], axis=AXIS.X, op=ALU.max)
+            nc.vector.tensor_tensor(
+                out=expd[:, :, ts],
+                in0=scores[:].rearrange("p t m -> p m t"),
+                in1=top[:].unsqueeze(1).to_broadcast([P, ROWS, HALF]),
+                op=ALU.subtract,
+            )
+            nc.scalar.activation(out=expd[:, :, ts], in_=expd[:, :, ts], func=ACT.Exp, scale=SCALE)
+            nc.vector.tensor_reduce(
+                out=sums[:, ts],
+                in_=expd[:, :, ts].rearrange("p m t -> p t m"),
+                axis=AXIS.X,
+                op=ALU.add,
+            )
+
+        exp_tok = keep.tile([P, ROWS * ROWS], F32, align_bytes=64, name="exp_tok")
+        nc.vector.transpose(out=exp_tok[:], in_=expd[:].rearrange("p m t -> p (m t)"))
+        sum_tok = keep.tile([P, ROWS], F32, align_bytes=64, name="sum_tok")
+        nc.vector.transpose(out=sum_tok[:], in_=sums[:])
+        inv_tok = keep.tile([P, ROWS], F32, name="inv_tok")
+        nc.vector.reciprocal(out=inv_tok[:], in_=sum_tok[:])
+
+        exp_view = exp_tok[:].rearrange("p (m i) -> p i m", i=ROWS)
+        att = []
+        for j in range(2):
+            part = slice(j * HEADS, (j + 1) * HEADS)
+            att_j = keep.tile([P, HEADS, HEADS], F32, name="att%d" % j)
+            nc.vector.tensor_tensor(
+                out=att_j[:],
+                in0=exp_view[:, part, part],
+                in1=inv_tok[:, part].unsqueeze(2).to_broadcast([P, HEADS, HEADS]),
+                op=ALU.mult,
+            )
+            att.append(att_j)
+        result = keep.tile([P, HEADS * HEADS], F32, name="result")
+        nc.vector.scalar_tensor_tensor(
+            out=result[:],
+            in0=att[1][:].rearrange("p a h -> p (a h)"),
+            scalar=neg_lam[:, 0:1],
+            in1=att[0][:].rearrange("p a h -> p (a h)"),
+            op0=ALU.mult,
+            op1=ALU.add,
+        )
+        nc.sync.dma_start(out=out.rearrange("b n a h -> (b n) (a h)"), in_=result[:])

@@ -23,9 +23,13 @@ ROWS = 2 * HEADS
 D = 32
 QUAD = 32
 QUADS = P // QUAD
-W_TILES = 4
-HALF = ROWS // 2
-Y_HALF = HEADS * D
+TILES = 8
+BANK = 512
+BANK_TILES = 2
+BANK_HEADS = 8
+LAG = 2
+CHUNK = 8
+CHUNKS = QUAD // CHUNK
 SCALE = D ** -0.5
 LAM_INIT = 0.8 - 0.6 * math.exp(-0.3 * 12)
 
@@ -42,37 +46,6 @@ def regroup_rows(nc, banks, ident, row_words, grouped_words):
     )
 
 
-def project(nc, stage, banks, ident, x_codes, x_scales, w_tiles, y_halves):
-    for s in range(W_TILES):
-        w_words = w_tiles[s][:].bitcast(F32)
-        grouped = stage.tile([P, 2 * PASSES * P * 4], BF16, align_bytes=64, name="grouped")
-        grouped_words = grouped[:].bitcast(F32)
-        for j in range(2):
-            regroup_rows(
-                nc,
-                banks,
-                ident,
-                w_words[:, j * WORDS : (j + 1) * WORDS],
-                grouped_words[:, j * WORDS : (j + 1) * WORDS],
-            )
-        w_codes = stage.tile([P, 2 * PASSES * P], U32, align_bytes=64, name="w_codes")
-        w_scales = stage.tile([P, 2 * PASSES * P], U8, align_bytes=64, name="w_scales")
-        nc.vector.quantize_mx(out=w_codes[:].bitcast(FP8X4), scales=w_scales[:], in_=grouped[:])
-        for j in range(2):
-            for g in range(PASSES):
-                x_cols = slice(g * P, (g + 1) * P)
-                w_cols = slice((j * PASSES + g) * P, (j * PASSES + g + 1) * P)
-                nc.tensor.matmul_mx(
-                    out=y_halves[j][:, s * P : (s + 1) * P],
-                    lhsT=x_codes[:, x_cols].bitcast(FP8X4),
-                    lhsT_scale=x_scales[:, x_cols],
-                    rhs=w_codes[:, w_cols].bitcast(FP8X4),
-                    rhs_scale=w_scales[:, w_cols],
-                    start=(g == 0),
-                    stop=(g == PASSES - 1),
-                )
-
-
 def tile_differentialattention_pa_s_kernel(tc, x, Wq, Wk, lq1, lq2, lk1, lk2, out):
     nc = tc.nc
     with ExitStack() as ctx:
@@ -80,17 +53,17 @@ def tile_differentialattention_pa_s_kernel(tc, x, Wq, Wk, lq1, lq2, lk1, lk2, ou
         stage = ctx.enter_context(tc.tile_pool(name="stage", bufs=3))
         banks = ctx.enter_context(tc.psum_pool(name="banks", bufs=4))
         y_pool = ctx.enter_context(tc.psum_pool(name="y_pool", bufs=1))
+        ctx.enter_context(tc.manual_schedule())
 
         x_sb = keep.tile([P, K], BF16, name="x_sb")
         nc.sync.dma_start(out=x_sb[:], in_=x.rearrange("b n k -> (b n) k"))
-        w_tiles = {}
-        for name, w in (("q", Wq), ("k", Wk)):
+        w_tiles = []
+        for w in (Wq, Wk):
             w_view = w.rearrange("(s p j) k -> s p (j k)", p=P, j=2)
-            w_tiles[name] = []
-            for s in range(W_TILES):
-                w_sb = keep.tile([P, 2 * K], BF16, name="w_%s%d" % (name, s))
+            for s in range(TILES // 2):
+                w_sb = keep.tile([P, 2 * K], BF16, name="w_sb%d" % len(w_tiles))
                 nc.sync.dma_start(out=w_sb[:], in_=w_view[s])
-                w_tiles[name].append(w_sb)
+                w_tiles.append(w_sb)
 
         lam_rows = keep.tile([P, 4 * D], BF16, name="lam_rows")
         nc.vector.memset(lam_rows[:], 0.0)
@@ -108,6 +81,7 @@ def tile_differentialattention_pa_s_kernel(tc, x, Wq, Wk, lq1, lq2, lk1, lk2, ou
         nc.scalar.activation(out=warm[:, 1:2], in_=warm[:, 0:1], func=ACT.Exp)
         q_blocks = keep.tile([P, QUAD, QUADS, ROWS], F32, name="q_blocks")
         nc.vector.memset(q_blocks[:], 0.0)
+        k_cols = keep.tile([P, QUAD, ROWS], F32, name="k_cols")
 
         x_grouped = keep.tile([P, PASSES * P * 4], BF16, align_bytes=64, name="x_grouped")
         regroup_rows(nc, banks, ident[:], x_sb[:].bitcast(F32), x_grouped[:].bitcast(F32))
@@ -140,84 +114,141 @@ def tile_differentialattention_pa_s_kernel(tc, x, Wq, Wk, lq1, lq2, lk1, lk2, ou
             op1=ALU.subtract,
         )
 
-        yq = [y_pool.tile([P, Y_HALF], F32, name="yq%d" % j) for j in range(2)]
-        project(nc, stage, banks, ident[:], x_codes, x_scales, w_tiles["q"], yq)
-        q_t = keep.tile([P, ROWS * QUAD], F32, align_bytes=64, name="q_t")
-        for j in range(2):
-            nc.vector.transpose(out=q_t[:, j * Y_HALF : (j + 1) * Y_HALF], in_=yq[j][:])
-        for c in range(QUADS):
-            rows = slice(c * QUAD, (c + 1) * QUAD)
-            source = q_t[rows, :].rearrange("p (i t) -> p t i", t=QUAD)
-            if c % 2 == 0:
-                nc.vector.tensor_copy(out=q_blocks[rows, :, c, :], in_=source)
-            else:
-                nc.gpsimd.tensor_scalar(
-                    out=q_blocks[rows, :, c, :],
-                    in0=source,
-                    scalar1=1.0,
-                    scalar2=0.0,
-                    op0=ALU.mult,
-                    op1=ALU.add,
+        y_banks = [y_pool.tile([P, BANK], F32, name="y_bank%d" % b) for b in range(4)]
+        grouped = {}
+        w_codes = {}
+        w_scales = {}
+
+        def regroup_tile(n):
+            grouped[n] = stage.tile([P, 2 * PASSES * P * 4], BF16, align_bytes=64, name="grouped")
+            for j in range(2):
+                words = slice(j * WORDS, (j + 1) * WORDS)
+                regroup_rows(
+                    nc,
+                    banks,
+                    ident[:],
+                    w_tiles[n][:].bitcast(F32)[:, words],
+                    grouped[n][:].bitcast(F32)[:, words],
                 )
 
-        yk = [y_pool.tile([P, Y_HALF], F32, name="yk%d" % j) for j in range(2)]
-        project(nc, stage, banks, ident[:], x_codes, x_scales, w_tiles["k"], yk)
-        k_t = keep.tile([P, ROWS * QUAD], F32, align_bytes=64, name="k_t")
-        for j in range(2):
-            nc.vector.transpose(out=k_t[:, j * Y_HALF : (j + 1) * Y_HALF], in_=yk[j][:])
-        k_cols = keep.tile([P, QUAD, ROWS], F32, name="k_cols")
-        k_t_view = k_t[:].rearrange("p (m t) -> p t m", t=QUAD)
-        nc.vector.tensor_copy(out=k_cols[:, 0:HALF, :], in_=k_t_view[:, 0:HALF, :])
-        nc.scalar.copy(out=k_cols[:, HALF:QUAD, :], in_=k_t_view[:, HALF:QUAD, :])
+        def quantise_tile(n):
+            w_codes[n] = stage.tile([P, 2 * PASSES * P], U32, align_bytes=64, name="w_codes")
+            w_scales[n] = stage.tile([P, 2 * PASSES * P], U8, align_bytes=64, name="w_scales")
+            nc.vector.quantize_mx(
+                out=w_codes[n][:].bitcast(FP8X4), scales=w_scales[n][:], in_=grouped[n][:]
+            )
 
-        expd = keep.tile([P, ROWS, QUAD], F32, align_bytes=64, name="expd")
-        sums = keep.tile([P, QUAD], F32, align_bytes=64, name="sums")
-        for half in range(2):
-            ts = slice(half * HALF, (half + 1) * HALF)
-            scores = banks.tile([P, HALF, ROWS], F32, tag="bank", name="scores")
-            for t in range(HALF):
+        def multiply_tile(n):
+            for j in range(2):
+                y_start = j * (BANK // 2) + (n % BANK_TILES) * P
+                for g in range(PASSES):
+                    x_cols = slice(g * P, (g + 1) * P)
+                    w_cols = slice((j * PASSES + g) * P, (j * PASSES + g + 1) * P)
+                    nc.tensor.matmul_mx(
+                        out=y_banks[n // BANK_TILES][:, y_start : y_start + P],
+                        lhsT=x_codes[:, x_cols].bitcast(FP8X4),
+                        lhsT_scale=x_scales[:, x_cols],
+                        rhs=w_codes[n][:, w_cols].bitcast(FP8X4),
+                        rhs_scale=w_scales[n][:, w_cols],
+                        start=(g == 0),
+                        stop=(g == PASSES - 1),
+                    )
+
+        def unpack_bank(b):
+            swapped = stage.tile([P, BANK], F32, align_bytes=64, name="swapped")
+            nc.vector.transpose(out=swapped[:], in_=y_banks[b][:])
+            heads = slice((b % 2) * BANK_HEADS, (b % 2 + 1) * BANK_HEADS)
+            if b < 2:
+                for c in range(QUADS):
+                    rows = slice(c * QUAD, (c + 1) * QUAD)
+                    source = swapped[rows, :].rearrange("p (j h t) -> p t j h", j=2, t=QUAD)
+                    target = q_blocks[rows, :, c, :].rearrange("p t (j h) -> p t j h", j=2)
+                    if c % 2 == 0:
+                        nc.vector.tensor_copy(out=target[:, :, :, heads], in_=source)
+                    else:
+                        nc.gpsimd.tensor_scalar(
+                            out=target[:, :, :, heads],
+                            in0=source,
+                            scalar1=1.0,
+                            scalar2=0.0,
+                            op0=ALU.mult,
+                            op1=ALU.add,
+                        )
+            else:
+                source = swapped[:].rearrange("p (j h t) -> p t j h", j=2, t=QUAD)
+                target = k_cols[:].rearrange("p t (j h) -> p t j h", j=2)
+                first = slice(0, QUAD // 2)
+                second = slice(QUAD // 2, QUAD)
+                nc.vector.tensor_copy(out=target[:, first, :, heads], in_=source[:, first])
+                nc.scalar.copy(out=target[:, second, :, heads], in_=source[:, second])
+
+        for step in range(TILES + LAG):
+            if step < TILES:
+                regroup_tile(step)
+            if 1 <= step <= TILES:
+                quantise_tile(step - 1)
+            if step >= LAG:
+                multiply_tile(step - LAG)
+                if (step - LAG) % BANK_TILES == BANK_TILES - 1:
+                    unpack_bank((step - LAG) // BANK_TILES)
+
+        scores = []
+        for chunk in range(CHUNKS):
+            scores.append(banks.tile([P, CHUNK, ROWS], F32, tag="bank", name="scores"))
+            for t in range(CHUNK):
                 nc.tensor.matmul(
-                    out=scores[:, t, :],
-                    lhsT=q_blocks[:, half * HALF + t].rearrange("p c i -> p (c i)"),
-                    rhs=k_cols[:, half * HALF + t, :],
+                    out=scores[chunk][:, t, :],
+                    lhsT=q_blocks[:, chunk * CHUNK + t].rearrange("p c i -> p (c i)"),
+                    rhs=k_cols[:, chunk * CHUNK + t, :],
                     start=True,
                     stop=True,
                 )
-            top = keep.tile([P, HALF], F32, name="top%d" % half)
-            nc.vector.tensor_reduce(out=top[:], in_=scores[:], axis=AXIS.X, op=ALU.max)
-            nc.vector.tensor_tensor(
-                out=expd[:, :, ts],
-                in0=scores[:].rearrange("p t m -> p m t"),
-                in1=top[:].unsqueeze(1).to_broadcast([P, ROWS, HALF]),
-                op=ALU.subtract,
-            )
-            nc.scalar.activation(out=expd[:, :, ts], in_=expd[:, :, ts], func=ACT.Exp, scale=SCALE)
-            nc.vector.tensor_reduce(
-                out=sums[:, ts],
-                in_=expd[:, :, ts].rearrange("p m t -> p t m"),
-                axis=AXIS.X,
-                op=ALU.add,
-            )
 
-        exp_tok = keep.tile([P, ROWS * ROWS], F32, align_bytes=64, name="exp_tok")
-        nc.vector.transpose(out=exp_tok[:], in_=expd[:].rearrange("p m t -> p (m t)"))
+        top = keep.tile([P, QUAD], F32, name="top")
+        expd = keep.tile([P, ROWS, QUAD], F32, align_bytes=64, name="expd")
+        sums = keep.tile([P, QUAD], F32, align_bytes=64, name="sums")
+        for chunk in range(CHUNKS + 1):
+            if chunk < CHUNKS:
+                ts = slice(chunk * CHUNK, (chunk + 1) * CHUNK)
+                nc.vector.tensor_reduce(
+                    out=top[:, ts], in_=scores[chunk][:], axis=AXIS.X, op=ALU.max
+                )
+                nc.vector.tensor_tensor(
+                    out=expd[:, :, ts],
+                    in0=scores[chunk][:].rearrange("p t m -> p m t"),
+                    in1=top[:, ts].unsqueeze(1).to_broadcast([P, ROWS, CHUNK]),
+                    op=ALU.subtract,
+                )
+                nc.scalar.activation(
+                    out=expd[:, :, ts], in_=expd[:, :, ts], func=ACT.Exp, scale=SCALE
+                )
+            if chunk >= 1:
+                ts = slice((chunk - 1) * CHUNK, chunk * CHUNK)
+                nc.vector.tensor_reduce(
+                    out=sums[:, ts],
+                    in_=expd[:, :, ts].rearrange("p m t -> p t m"),
+                    axis=AXIS.X,
+                    op=ALU.add,
+                )
+
         sum_tok = keep.tile([P, ROWS], F32, align_bytes=64, name="sum_tok")
         nc.vector.transpose(out=sum_tok[:], in_=sums[:])
         inv_tok = keep.tile([P, ROWS], F32, name="inv_tok")
         nc.vector.reciprocal(out=inv_tok[:], in_=sum_tok[:])
+        exp_tok = keep.tile([P, ROWS * ROWS], F32, align_bytes=64, name="exp_tok")
+        nc.vector.transpose(out=exp_tok[:], in_=expd[:].rearrange("p m t -> p (m t)"))
 
         exp_view = exp_tok[:].rearrange("p (m i) -> p i m", i=ROWS)
         att = []
         for j in range(2):
             part = slice(j * HEADS, (j + 1) * HEADS)
-            att_j = keep.tile([P, HEADS, HEADS], F32, name="att%d" % j)
+            att.append(keep.tile([P, HEADS, HEADS], F32, name="att%d" % j))
             nc.vector.tensor_tensor(
-                out=att_j[:],
+                out=att[j][:],
                 in0=exp_view[:, part, part],
                 in1=inv_tok[:, part].unsqueeze(2).to_broadcast([P, HEADS, HEADS]),
                 op=ALU.mult,
             )
-            att.append(att_j)
         result = keep.tile([P, HEADS * HEADS], F32, name="result")
         nc.vector.scalar_tensor_tensor(
             out=result[:],

@@ -8,6 +8,7 @@ F32 = mybir.dt.float32
 BF16 = mybir.dt.bfloat16
 U32 = mybir.dt.uint32
 U8 = mybir.dt.uint8
+I32 = mybir.dt.int32
 FP8X4 = mybir.dt.float8_e4m3fn_x4
 ALU = mybir.AluOpType
 ACT = mybir.ActivationFunctionType
@@ -30,6 +31,8 @@ BANK_HEADS = 8
 LAG = 2
 CHUNK = 8
 CHUNKS = QUAD // CHUNK
+KICK = 4
+SCORE_COLS = 44
 SCALE = D ** -0.5
 LAM_INIT = 0.8 - 0.6 * math.exp(-0.3 * 12)
 
@@ -54,6 +57,29 @@ def tile_differentialattention_pa_s_kernel(tc, x, Wq, Wk, lq1, lq2, lk1, lk2, ou
         banks = ctx.enter_context(tc.psum_pool(name="banks", bufs=4))
         y_pool = ctx.enter_context(tc.psum_pool(name="y_pool", bufs=1))
         ctx.enter_context(tc.manual_schedule())
+
+        idle_codes = keep.tile([P, BANK], U32, align_bytes=64, name="idle_codes")
+        idle_scales = keep.tile([P, BANK], U8, align_bytes=64, name="idle_scales")
+        idle_zeros = keep.tile([P, 4 * BANK], BF16, align_bytes=64, name="idle_zeros")
+        nc.vector.memset(idle_zeros[:].bitcast(I32), 0)
+        nc.vector.quantize_mx(
+            out=idle_codes[:].bitcast(FP8X4), scales=idle_scales[:], in_=idle_zeros[:]
+        )
+        y_banks = [y_pool.tile([P, BANK], F32, name="y_bank%d" % b) for b in range(4)]
+
+        def hold_clock(passes):
+            for repeat in range(passes):
+                nc.tensor.matmul_mx(
+                    out=y_banks[3][:],
+                    lhsT=idle_codes[:, 0:P].bitcast(FP8X4),
+                    lhsT_scale=idle_scales[:, 0:P],
+                    rhs=idle_codes[:].bitcast(FP8X4),
+                    rhs_scale=idle_scales[:],
+                    start=True,
+                    stop=True,
+                )
+
+        hold_clock(KICK)
 
         x_sb = keep.tile([P, K], BF16, name="x_sb")
         nc.sync.dma_start(out=x_sb[:], in_=x.rearrange("b n k -> (b n) k"))
@@ -81,7 +107,8 @@ def tile_differentialattention_pa_s_kernel(tc, x, Wq, Wk, lq1, lq2, lk1, lk2, ou
         nc.scalar.activation(out=warm[:, 1:2], in_=warm[:, 0:1], func=ACT.Exp)
         q_blocks = keep.tile([P, QUAD, QUADS, ROWS], F32, name="q_blocks")
         nc.vector.memset(q_blocks[:], 0.0)
-        k_cols = keep.tile([P, QUAD, ROWS], F32, name="k_cols")
+        k_cols = keep.tile([P, QUAD + 1, ROWS], F32, name="k_cols")
+        nc.vector.memset(k_cols[:, QUAD, :], 0.0)
 
         x_grouped = keep.tile([P, PASSES * P * 4], BF16, align_bytes=64, name="x_grouped")
         regroup_rows(nc, banks, ident[:], x_sb[:].bitcast(F32), x_grouped[:].bitcast(F32))
@@ -114,7 +141,6 @@ def tile_differentialattention_pa_s_kernel(tc, x, Wq, Wk, lq1, lq2, lk1, lk2, ou
             op1=ALU.subtract,
         )
 
-        y_banks = [y_pool.tile([P, BANK], F32, name="y_bank%d" % b) for b in range(4)]
         grouped = {}
         w_codes = {}
         w_scales = {}
@@ -176,7 +202,7 @@ def tile_differentialattention_pa_s_kernel(tc, x, Wq, Wk, lq1, lq2, lk1, lk2, ou
                         )
             else:
                 source = swapped[:].rearrange("p (j h t) -> p t j h", j=2, t=QUAD)
-                target = k_cols[:].rearrange("p t (j h) -> p t j h", j=2)
+                target = k_cols[:, 0:QUAD, :].rearrange("p t (j h) -> p t j h", j=2)
                 first = slice(0, QUAD // 2)
                 second = slice(QUAD // 2, QUAD)
                 nc.vector.tensor_copy(out=target[:, first, :, heads], in_=source[:, first])
@@ -187,19 +213,23 @@ def tile_differentialattention_pa_s_kernel(tc, x, Wq, Wk, lq1, lq2, lk1, lk2, ou
                 regroup_tile(step)
             if 1 <= step <= TILES:
                 quantise_tile(step - 1)
-            if step >= LAG:
+            if step < LAG:
+                hold_clock(1)
+            else:
                 multiply_tile(step - LAG)
                 if (step - LAG) % BANK_TILES == BANK_TILES - 1:
                     unpack_bank((step - LAG) // BANK_TILES)
 
+        k_flat = k_cols[:].rearrange("p t m -> p (t m)")
         scores = []
         for chunk in range(CHUNKS):
-            scores.append(banks.tile([P, CHUNK, ROWS], F32, tag="bank", name="scores"))
+            scores.append(banks.tile([P, CHUNK, SCORE_COLS], F32, tag="bank", name="scores"))
             for t in range(CHUNK):
+                first_col = (chunk * CHUNK + t) * ROWS
                 nc.tensor.matmul(
                     out=scores[chunk][:, t, :],
                     lhsT=q_blocks[:, chunk * CHUNK + t].rearrange("p c i -> p (c i)"),
-                    rhs=k_cols[:, chunk * CHUNK + t, :],
+                    rhs=k_flat[:, first_col : first_col + SCORE_COLS],
                     start=True,
                     stop=True,
                 )
@@ -211,11 +241,11 @@ def tile_differentialattention_pa_s_kernel(tc, x, Wq, Wk, lq1, lq2, lk1, lk2, ou
             if chunk < CHUNKS:
                 ts = slice(chunk * CHUNK, (chunk + 1) * CHUNK)
                 nc.vector.tensor_reduce(
-                    out=top[:, ts], in_=scores[chunk][:], axis=AXIS.X, op=ALU.max
+                    out=top[:, ts], in_=scores[chunk][:, :, 0:ROWS], axis=AXIS.X, op=ALU.max
                 )
                 nc.vector.tensor_tensor(
                     out=expd[:, :, ts],
-                    in0=scores[chunk][:].rearrange("p t m -> p m t"),
+                    in0=scores[chunk][:, :, 0:ROWS].rearrange("p t m -> p m t"),
                     in1=top[:, ts].unsqueeze(1).to_broadcast([P, ROWS, CHUNK]),
                     op=ALU.subtract,
                 )

@@ -8,7 +8,6 @@ F32 = mybir.dt.float32
 BF16 = mybir.dt.bfloat16
 U32 = mybir.dt.uint32
 U8 = mybir.dt.uint8
-I32 = mybir.dt.int32
 FP8X4 = mybir.dt.float8_e4m3fn_x4
 ALU = mybir.AluOpType
 ACT = mybir.ActivationFunctionType
@@ -31,8 +30,6 @@ BANK_HEADS = 8
 LAG = 2
 CHUNK = 8
 CHUNKS = QUAD // CHUNK
-KICK = 4
-SCORE_COLS = 44
 SCALE = D ** -0.5
 LAM_INIT = 0.8 - 0.6 * math.exp(-0.3 * 12)
 
@@ -57,29 +54,6 @@ def tile_differentialattention_pa_s_kernel(tc, x, Wq, Wk, lq1, lq2, lk1, lk2, ou
         banks = ctx.enter_context(tc.psum_pool(name="banks", bufs=4))
         y_pool = ctx.enter_context(tc.psum_pool(name="y_pool", bufs=1))
         ctx.enter_context(tc.manual_schedule())
-
-        idle_codes = keep.tile([P, BANK], U32, align_bytes=64, name="idle_codes")
-        idle_scales = keep.tile([P, BANK], U8, align_bytes=64, name="idle_scales")
-        idle_zeros = keep.tile([P, 4 * BANK], BF16, align_bytes=64, name="idle_zeros")
-        nc.vector.memset(idle_zeros[:].bitcast(I32), 0)
-        nc.vector.quantize_mx(
-            out=idle_codes[:].bitcast(FP8X4), scales=idle_scales[:], in_=idle_zeros[:]
-        )
-        y_banks = [y_pool.tile([P, BANK], F32, name="y_bank%d" % b) for b in range(4)]
-
-        def hold_clock(passes):
-            for repeat in range(passes):
-                nc.tensor.matmul_mx(
-                    out=y_banks[3][:],
-                    lhsT=idle_codes[:, 0:P].bitcast(FP8X4),
-                    lhsT_scale=idle_scales[:, 0:P],
-                    rhs=idle_codes[:].bitcast(FP8X4),
-                    rhs_scale=idle_scales[:],
-                    start=True,
-                    stop=True,
-                )
-
-        hold_clock(KICK)
 
         x_sb = keep.tile([P, K], BF16, name="x_sb")
         nc.sync.dma_start(out=x_sb[:], in_=x.rearrange("b n k -> (b n) k"))
@@ -107,8 +81,7 @@ def tile_differentialattention_pa_s_kernel(tc, x, Wq, Wk, lq1, lq2, lk1, lk2, ou
         nc.scalar.activation(out=warm[:, 1:2], in_=warm[:, 0:1], func=ACT.Exp)
         q_blocks = keep.tile([P, QUAD, QUADS, ROWS], F32, name="q_blocks")
         nc.vector.memset(q_blocks[:], 0.0)
-        k_cols = keep.tile([P, QUAD + 1, ROWS], F32, name="k_cols")
-        nc.vector.memset(k_cols[:, QUAD, :], 0.0)
+        k_cols = keep.tile([P, QUAD, ROWS], F32, name="k_cols")
 
         x_grouped = keep.tile([P, PASSES * P * 4], BF16, align_bytes=64, name="x_grouped")
         regroup_rows(nc, banks, ident[:], x_sb[:].bitcast(F32), x_grouped[:].bitcast(F32))
@@ -141,6 +114,7 @@ def tile_differentialattention_pa_s_kernel(tc, x, Wq, Wk, lq1, lq2, lk1, lk2, ou
             op1=ALU.subtract,
         )
 
+        y_banks = [y_pool.tile([P, BANK], F32, name="y_bank%d" % b) for b in range(4)]
         grouped = {}
         w_codes = {}
         w_scales = {}
@@ -202,7 +176,7 @@ def tile_differentialattention_pa_s_kernel(tc, x, Wq, Wk, lq1, lq2, lk1, lk2, ou
                         )
             else:
                 source = swapped[:].rearrange("p (j h t) -> p t j h", j=2, t=QUAD)
-                target = k_cols[:, 0:QUAD, :].rearrange("p t (j h) -> p t j h", j=2)
+                target = k_cols[:].rearrange("p t (j h) -> p t j h", j=2)
                 first = slice(0, QUAD // 2)
                 second = slice(QUAD // 2, QUAD)
                 nc.vector.tensor_copy(out=target[:, first, :, heads], in_=source[:, first])
@@ -213,23 +187,28 @@ def tile_differentialattention_pa_s_kernel(tc, x, Wq, Wk, lq1, lq2, lk1, lk2, ou
                 regroup_tile(step)
             if 1 <= step <= TILES:
                 quantise_tile(step - 1)
-            if step < LAG:
-                hold_clock(1)
-            else:
+            if step >= LAG:
                 multiply_tile(step - LAG)
                 if (step - LAG) % BANK_TILES == BANK_TILES - 1:
                     unpack_bank((step - LAG) // BANK_TILES)
 
-        k_flat = k_cols[:].rearrange("p t m -> p (t m)")
         scores = []
+        probe = banks.tile([P, 12, ROWS], F32, tag="bank", name="probe")
+        for t in range(12):
+            nc.tensor.matmul(
+                out=probe[:, t, :],
+                lhsT=q_blocks[:, t].rearrange("p c i -> p (c i)"),
+                rhs=k_cols[:, t, :],
+                start=True,
+                stop=True,
+            )
         for chunk in range(CHUNKS):
-            scores.append(banks.tile([P, CHUNK, SCORE_COLS], F32, tag="bank", name="scores"))
+            scores.append(banks.tile([P, CHUNK, ROWS], F32, tag="bank", name="scores"))
             for t in range(CHUNK):
-                first_col = (chunk * CHUNK + t) * ROWS
                 nc.tensor.matmul(
                     out=scores[chunk][:, t, :],
                     lhsT=q_blocks[:, chunk * CHUNK + t].rearrange("p c i -> p (c i)"),
-                    rhs=k_flat[:, first_col : first_col + SCORE_COLS],
+                    rhs=k_cols[:, chunk * CHUNK + t, :],
                     start=True,
                     stop=True,
                 )
@@ -241,11 +220,11 @@ def tile_differentialattention_pa_s_kernel(tc, x, Wq, Wk, lq1, lq2, lk1, lk2, ou
             if chunk < CHUNKS:
                 ts = slice(chunk * CHUNK, (chunk + 1) * CHUNK)
                 nc.vector.tensor_reduce(
-                    out=top[:, ts], in_=scores[chunk][:, :, 0:ROWS], axis=AXIS.X, op=ALU.max
+                    out=top[:, ts], in_=scores[chunk][:], axis=AXIS.X, op=ALU.max
                 )
                 nc.vector.tensor_tensor(
                     out=expd[:, :, ts],
-                    in0=scores[chunk][:, :, 0:ROWS].rearrange("p t m -> p m t"),
+                    in0=scores[chunk][:].rearrange("p t m -> p m t"),
                     in1=top[:, ts].unsqueeze(1).to_broadcast([P, ROWS, CHUNK]),
                     op=ALU.subtract,
                 )

@@ -8,6 +8,7 @@ F32 = mybir.dt.float32
 BF16 = mybir.dt.bfloat16
 U32 = mybir.dt.uint32
 U8 = mybir.dt.uint8
+I32 = mybir.dt.int32
 FP8X4 = mybir.dt.float8_e4m3fn_x4
 ALU = mybir.AluOpType
 ACT = mybir.ActivationFunctionType
@@ -23,15 +24,17 @@ ROWS = 2 * HEADS
 D = 32
 QUAD = 32
 QUADS = P // QUAD
-TILES = 8
 BANK = 512
-BANK_TILES = 2
-BANK_HEADS = 8
-LAG = 2
+W_TILES = 4
+PAIRS = 4
+PAIR_HEADS = 8
 CHUNK = 8
 CHUNKS = QUAD // CHUNK
 SCALE = D ** -0.5
 LAM_INIT = 0.8 - 0.6 * math.exp(-0.3 * 12)
+IDLE = 4
+BURST = 16
+SCORE_COLS = 44
 
 FLOPS = 2 * P * K * 2 * K + 2 * P * ROWS * ROWS * D
 
@@ -50,9 +53,10 @@ def tile_differentialattention_pa_s_kernel(tc, x, Wq, Wk, lq1, lq2, lk1, lk2, ou
     nc = tc.nc
     with ExitStack() as ctx:
         keep = ctx.enter_context(tc.tile_pool(name="keep", bufs=1))
-        stage = ctx.enter_context(tc.tile_pool(name="stage", bufs=3))
-        banks = ctx.enter_context(tc.psum_pool(name="banks", bufs=4))
-        y_pool = ctx.enter_context(tc.psum_pool(name="y_pool", bufs=1))
+        stage = ctx.enter_context(tc.tile_pool(name="stage", bufs=4))
+        banks = ctx.enter_context(tc.psum_pool(name="banks", bufs=5))
+        y_pool = ctx.enter_context(tc.psum_pool(name="y_pool", bufs=2))
+        idle_pool = ctx.enter_context(tc.psum_pool(name="idle_pool", bufs=1))
         ctx.enter_context(tc.manual_schedule())
 
         x_sb = keep.tile([P, K], BF16, name="x_sb")
@@ -60,7 +64,7 @@ def tile_differentialattention_pa_s_kernel(tc, x, Wq, Wk, lq1, lq2, lk1, lk2, ou
         w_tiles = []
         for w in (Wq, Wk):
             w_view = w.rearrange("(s p j) k -> s p (j k)", p=P, j=2)
-            for s in range(TILES // 2):
+            for s in range(W_TILES):
                 w_sb = keep.tile([P, 2 * K], BF16, name="w_sb%d" % len(w_tiles))
                 nc.sync.dma_start(out=w_sb[:], in_=w_view[s])
                 w_tiles.append(w_sb)
@@ -79,15 +83,118 @@ def tile_differentialattention_pa_s_kernel(tc, x, Wq, Wk, lq1, lq2, lk1, lk2, ou
         warm = keep.tile([P, 2], F32, name="warm")
         nc.vector.memset(warm[:], 0.0)
         nc.scalar.activation(out=warm[:, 1:2], in_=warm[:, 0:1], func=ACT.Exp)
+        idle_zeros = keep.tile([P, 4 * P], BF16, align_bytes=64, name="idle_zeros")
+        idle_codes = keep.tile([P, P], U32, align_bytes=64, name="idle_codes")
+        idle_scales = keep.tile([P, P], U8, align_bytes=64, name="idle_scales")
+        nc.vector.memset(idle_zeros[:].bitcast(I32), 0)
+        nc.vector.quantize_mx(
+            out=idle_codes[:].bitcast(FP8X4), scales=idle_scales[:], in_=idle_zeros[:]
+        )
+        idle_bank = idle_pool.tile([P, P], F32, name="idle_bank")
+
+        def hold_clock(passes):
+            for repeat in range(passes):
+                nc.tensor.matmul_mx(
+                    out=idle_bank[:],
+                    lhsT=idle_codes[:].bitcast(FP8X4),
+                    lhsT_scale=idle_scales[:],
+                    rhs=idle_codes[:].bitcast(FP8X4),
+                    rhs_scale=idle_scales[:],
+                    start=True,
+                    stop=True,
+                )
+
         q_blocks = keep.tile([P, QUAD, QUADS, ROWS], F32, name="q_blocks")
         nc.vector.memset(q_blocks[:], 0.0)
-        k_cols = keep.tile([P, QUAD, ROWS], F32, name="k_cols")
+        k_cols = keep.tile([P, QUAD + 1, ROWS], F32, name="k_cols")
+        nc.vector.memset(k_cols[:, QUAD, :], 0.0)
 
         x_grouped = keep.tile([P, PASSES * P * 4], BF16, align_bytes=64, name="x_grouped")
         regroup_rows(nc, banks, ident[:], x_sb[:].bitcast(F32), x_grouped[:].bitcast(F32))
         x_codes = keep.tile([P, PASSES * P], U32, align_bytes=64, name="x_codes")
         x_scales = keep.tile([P, PASSES * P], U8, align_bytes=64, name="x_scales")
         nc.vector.quantize_mx(out=x_codes[:].bitcast(FP8X4), scales=x_scales[:], in_=x_grouped[:])
+
+        grouped = {}
+        w_codes = {}
+        w_scales = {}
+
+        def regroup_tile(n):
+            grouped[n] = stage.tile([P, 2 * PASSES * P * 4], BF16, align_bytes=64, name="grouped")
+            for j in range(2):
+                words = slice(j * WORDS, (j + 1) * WORDS)
+                regroup_rows(
+                    nc,
+                    banks,
+                    ident[:],
+                    w_tiles[n][:].bitcast(F32)[:, words],
+                    grouped[n][:].bitcast(F32)[:, words],
+                )
+
+        def quantise_tile(n):
+            w_codes[n] = stage.tile([P, 2 * PASSES * P], U32, align_bytes=64, name="w_codes")
+            w_scales[n] = stage.tile([P, 2 * PASSES * P], U8, align_bytes=64, name="w_scales")
+            nc.vector.quantize_mx(
+                out=w_codes[n][:].bitcast(FP8X4), scales=w_scales[n][:], in_=grouped[n][:]
+            )
+
+        def multiply_tile(n, y_bank):
+            for j in range(2):
+                y_start = j * (BANK // 2) + (n % 2) * P
+                for g in range(PASSES):
+                    x_cols = slice(g * P, (g + 1) * P)
+                    w_cols = slice((j * PASSES + g) * P, (j * PASSES + g + 1) * P)
+                    nc.tensor.matmul_mx(
+                        out=y_bank[:, y_start : y_start + P],
+                        lhsT=x_codes[:, x_cols].bitcast(FP8X4),
+                        lhsT_scale=x_scales[:, x_cols],
+                        rhs=w_codes[n][:, w_cols].bitcast(FP8X4),
+                        rhs_scale=w_scales[n][:, w_cols],
+                        start=(g == 0),
+                        stop=(g == PASSES - 1),
+                    )
+            hold_clock(IDLE)
+
+        def unpack_bank(pair, y_bank):
+            swapped = stage.tile([P, BANK], F32, align_bytes=64, name="swapped")
+            nc.vector.transpose(out=swapped[:], in_=y_bank[:])
+            heads = slice((pair % 2) * PAIR_HEADS, (pair % 2 + 1) * PAIR_HEADS)
+            if pair < PAIRS // 2:
+                for c in range(QUADS):
+                    rows = slice(c * QUAD, (c + 1) * QUAD)
+                    source = swapped[rows, :].rearrange("p (j h t) -> p t j h", j=2, t=QUAD)
+                    target = q_blocks[rows, :, c, :].rearrange("p t (j h) -> p t j h", j=2)
+                    if c % 2 == 0:
+                        nc.vector.tensor_copy(out=target[:, :, :, heads], in_=source)
+                    else:
+                        nc.gpsimd.tensor_scalar(
+                            out=target[:, :, :, heads],
+                            in0=source,
+                            scalar1=1.0,
+                            scalar2=0.0,
+                            op0=ALU.mult,
+                            op1=ALU.add,
+                        )
+            else:
+                source = swapped[:].rearrange("p (j h t) -> p t j h", j=2, t=QUAD)
+                target = k_cols[:, 0:QUAD, :].rearrange("p t (j h) -> p t j h", j=2)
+                first = slice(0, QUAD // 2)
+                second = slice(QUAD // 2, QUAD)
+                nc.vector.tensor_copy(out=target[:, first, :, heads], in_=source[:, first])
+                nc.scalar.copy(out=target[:, second, :, heads], in_=source[:, second])
+
+        for pair in range(PAIRS + 1):
+            if pair < PAIRS:
+                regroup_tile(2 * pair)
+                regroup_tile(2 * pair + 1)
+            if pair >= 1:
+                quantise_tile(2 * pair - 2)
+                quantise_tile(2 * pair - 1)
+                y_bank = y_pool.tile([P, BANK], F32, tag="y_bank", name="y_bank")
+                multiply_tile(2 * pair - 2, y_bank)
+                multiply_tile(2 * pair - 1, y_bank)
+                unpack_bank(pair - 1, y_bank)
+        hold_clock(BURST)
 
         lam_bank = banks.tile([P, 4 * D], F32, tag="bank", name="lam_bank")
         nc.tensor.matmul(out=lam_bank[:], lhsT=ones[:], rhs=lam_rows[:], start=True, stop=True)
@@ -114,117 +221,33 @@ def tile_differentialattention_pa_s_kernel(tc, x, Wq, Wk, lq1, lq2, lk1, lk2, ou
             op1=ALU.subtract,
         )
 
-        y_banks = [y_pool.tile([P, BANK], F32, name="y_bank%d" % b) for b in range(4)]
-        grouped = {}
-        w_codes = {}
-        w_scales = {}
-
-        def regroup_tile(n):
-            grouped[n] = stage.tile([P, 2 * PASSES * P * 4], BF16, align_bytes=64, name="grouped")
-            for j in range(2):
-                words = slice(j * WORDS, (j + 1) * WORDS)
-                regroup_rows(
-                    nc,
-                    banks,
-                    ident[:],
-                    w_tiles[n][:].bitcast(F32)[:, words],
-                    grouped[n][:].bitcast(F32)[:, words],
-                )
-
-        def quantise_tile(n):
-            w_codes[n] = stage.tile([P, 2 * PASSES * P], U32, align_bytes=64, name="w_codes")
-            w_scales[n] = stage.tile([P, 2 * PASSES * P], U8, align_bytes=64, name="w_scales")
-            nc.vector.quantize_mx(
-                out=w_codes[n][:].bitcast(FP8X4), scales=w_scales[n][:], in_=grouped[n][:]
-            )
-
-        def multiply_tile(n):
-            for j in range(2):
-                y_start = j * (BANK // 2) + (n % BANK_TILES) * P
-                for g in range(PASSES):
-                    x_cols = slice(g * P, (g + 1) * P)
-                    w_cols = slice((j * PASSES + g) * P, (j * PASSES + g + 1) * P)
-                    nc.tensor.matmul_mx(
-                        out=y_banks[n // BANK_TILES][:, y_start : y_start + P],
-                        lhsT=x_codes[:, x_cols].bitcast(FP8X4),
-                        lhsT_scale=x_scales[:, x_cols],
-                        rhs=w_codes[n][:, w_cols].bitcast(FP8X4),
-                        rhs_scale=w_scales[n][:, w_cols],
-                        start=(g == 0),
-                        stop=(g == PASSES - 1),
-                    )
-
-        def unpack_bank(b):
-            swapped = stage.tile([P, BANK], F32, align_bytes=64, name="swapped")
-            nc.vector.transpose(out=swapped[:], in_=y_banks[b][:])
-            heads = slice((b % 2) * BANK_HEADS, (b % 2 + 1) * BANK_HEADS)
-            if b < 2:
-                for c in range(QUADS):
-                    rows = slice(c * QUAD, (c + 1) * QUAD)
-                    source = swapped[rows, :].rearrange("p (j h t) -> p t j h", j=2, t=QUAD)
-                    target = q_blocks[rows, :, c, :].rearrange("p t (j h) -> p t j h", j=2)
-                    if c % 2 == 0:
-                        nc.vector.tensor_copy(out=target[:, :, :, heads], in_=source)
-                    else:
-                        nc.gpsimd.tensor_scalar(
-                            out=target[:, :, :, heads],
-                            in0=source,
-                            scalar1=1.0,
-                            scalar2=0.0,
-                            op0=ALU.mult,
-                            op1=ALU.add,
-                        )
-            else:
-                source = swapped[:].rearrange("p (j h t) -> p t j h", j=2, t=QUAD)
-                target = k_cols[:].rearrange("p t (j h) -> p t j h", j=2)
-                first = slice(0, QUAD // 2)
-                second = slice(QUAD // 2, QUAD)
-                nc.vector.tensor_copy(out=target[:, first, :, heads], in_=source[:, first])
-                nc.scalar.copy(out=target[:, second, :, heads], in_=source[:, second])
-
-        for step in range(TILES + LAG):
-            if step < TILES:
-                regroup_tile(step)
-            if 1 <= step <= TILES:
-                quantise_tile(step - 1)
-            if step >= LAG:
-                multiply_tile(step - LAG)
-                if (step - LAG) % BANK_TILES == BANK_TILES - 1:
-                    unpack_bank((step - LAG) // BANK_TILES)
-
+        k_flat = k_cols[:].rearrange("p t m -> p (t m)")
         scores = []
-        probe = banks.tile([P, 12, ROWS], F32, tag="bank", name="probe")
-        for t in range(12):
-            nc.tensor.matmul(
-                out=probe[:, t, :],
-                lhsT=q_blocks[:, t].rearrange("p c i -> p (c i)"),
-                rhs=k_cols[:, t, :],
-                start=True,
-                stop=True,
-            )
         for chunk in range(CHUNKS):
-            scores.append(banks.tile([P, CHUNK, ROWS], F32, tag="bank", name="scores"))
+            scores.append(banks.tile([P, CHUNK, SCORE_COLS], F32, tag="bank", name="scores"))
             for t in range(CHUNK):
+                first_col = (chunk * CHUNK + t) * ROWS
                 nc.tensor.matmul(
                     out=scores[chunk][:, t, :],
                     lhsT=q_blocks[:, chunk * CHUNK + t].rearrange("p c i -> p (c i)"),
-                    rhs=k_cols[:, chunk * CHUNK + t, :],
+                    rhs=k_flat[:, first_col : first_col + SCORE_COLS],
                     start=True,
                     stop=True,
                 )
 
         top = keep.tile([P, QUAD], F32, name="top")
         expd = keep.tile([P, ROWS, QUAD], F32, align_bytes=64, name="expd")
-        sums = keep.tile([P, QUAD], F32, align_bytes=64, name="sums")
+        sums = keep.tile([P, QUAD], F32, name="sums")
+        inverse = keep.tile([P, QUAD], F32, name="inverse")
         for chunk in range(CHUNKS + 1):
             if chunk < CHUNKS:
                 ts = slice(chunk * CHUNK, (chunk + 1) * CHUNK)
                 nc.vector.tensor_reduce(
-                    out=top[:, ts], in_=scores[chunk][:], axis=AXIS.X, op=ALU.max
+                    out=top[:, ts], in_=scores[chunk][:, :, 0:ROWS], axis=AXIS.X, op=ALU.max
                 )
                 nc.vector.tensor_tensor(
                     out=expd[:, :, ts],
-                    in0=scores[chunk][:].rearrange("p t m -> p m t"),
+                    in0=scores[chunk][:, :, 0:ROWS].rearrange("p t m -> p m t"),
                     in1=top[:, ts].unsqueeze(1).to_broadcast([P, ROWS, CHUNK]),
                     op=ALU.subtract,
                 )
@@ -239,32 +262,27 @@ def tile_differentialattention_pa_s_kernel(tc, x, Wq, Wk, lq1, lq2, lk1, lk2, ou
                     axis=AXIS.X,
                     op=ALU.add,
                 )
+                nc.vector.reciprocal(out=inverse[:, ts], in_=sums[:, ts])
+                nc.vector.tensor_tensor(
+                    out=expd[:, :, ts],
+                    in0=expd[:, :, ts],
+                    in1=inverse[:, ts].unsqueeze(1).to_broadcast([P, ROWS, CHUNK]),
+                    op=ALU.mult,
+                )
 
-        sum_tok = keep.tile([P, ROWS], F32, align_bytes=64, name="sum_tok")
-        nc.vector.transpose(out=sum_tok[:], in_=sums[:])
-        inv_tok = keep.tile([P, ROWS], F32, name="inv_tok")
-        nc.vector.reciprocal(out=inv_tok[:], in_=sum_tok[:])
-        exp_tok = keep.tile([P, ROWS * ROWS], F32, align_bytes=64, name="exp_tok")
-        nc.vector.transpose(out=exp_tok[:], in_=expd[:].rearrange("p m t -> p (m t)"))
+        att = keep.tile([P, ROWS * ROWS], F32, align_bytes=64, name="att")
+        nc.vector.transpose(out=att[:], in_=expd[:].rearrange("p m t -> p (m t)"))
 
-        exp_view = exp_tok[:].rearrange("p (m i) -> p i m", i=ROWS)
-        att = []
-        for j in range(2):
-            part = slice(j * HEADS, (j + 1) * HEADS)
-            att.append(keep.tile([P, HEADS, HEADS], F32, name="att%d" % j))
-            nc.vector.tensor_tensor(
-                out=att[j][:],
-                in0=exp_view[:, part, part],
-                in1=inv_tok[:, part].unsqueeze(2).to_broadcast([P, HEADS, HEADS]),
-                op=ALU.mult,
-            )
-        result = keep.tile([P, HEADS * HEADS], F32, name="result")
+        att_view = att[:].rearrange("p (m i) -> p i m", i=ROWS)
+        result = keep.tile([P, HEADS, HEADS], F32, name="result")
         nc.vector.scalar_tensor_tensor(
             out=result[:],
-            in0=att[1][:].rearrange("p a h -> p (a h)"),
+            in0=att_view[:, HEADS:ROWS, HEADS:ROWS],
             scalar=neg_lam[:, 0:1],
-            in1=att[0][:].rearrange("p a h -> p (a h)"),
+            in1=att_view[:, 0:HEADS, 0:HEADS],
             op0=ALU.mult,
             op1=ALU.add,
         )
-        nc.sync.dma_start(out=out.rearrange("b n a h -> (b n) (a h)"), in_=result[:])
+        nc.sync.dma_start(
+            out=out.rearrange("b n a h -> (b n) (a h)"), in_=result[:].rearrange("p a h -> p (a h)")
+        )

@@ -32,7 +32,6 @@ CHUNK = 8
 CHUNKS = QUAD // CHUNK
 SCALE = D ** -0.5
 LAM_INIT = 0.8 - 0.6 * math.exp(-0.3 * 12)
-IDLE = 4
 BURST = 16
 SCORE_COLS = 44
 
@@ -153,7 +152,6 @@ def tile_differentialattention_pa_s_kernel(tc, x, Wq, Wk, lq1, lq2, lk1, lk2, ou
                         start=(g == 0),
                         stop=(g == PASSES - 1),
                     )
-            hold_clock(IDLE)
 
         def unpack_bank(pair, y_bank):
             swapped = stage.tile([P, BANK], F32, align_bytes=64, name="swapped")
@@ -183,17 +181,18 @@ def tile_differentialattention_pa_s_kernel(tc, x, Wq, Wk, lq1, lq2, lk1, lk2, ou
                 nc.vector.tensor_copy(out=target[:, first, :, heads], in_=source[:, first])
                 nc.scalar.copy(out=target[:, second, :, heads], in_=source[:, second])
 
-        for pair in range(PAIRS + 1):
-            if pair < PAIRS:
-                regroup_tile(2 * pair)
-                regroup_tile(2 * pair + 1)
-            if pair >= 1:
-                quantise_tile(2 * pair - 2)
-                quantise_tile(2 * pair - 1)
+        for weight in range(2):
+            tiles = range(weight * W_TILES, (weight + 1) * W_TILES)
+            for n in tiles:
+                regroup_tile(n)
+                if n > tiles[0]:
+                    quantise_tile(n - 1)
+            quantise_tile(tiles[-1])
+            for pair in (2 * weight, 2 * weight + 1):
                 y_bank = y_pool.tile([P, BANK], F32, tag="y_bank", name="y_bank")
-                multiply_tile(2 * pair - 2, y_bank)
-                multiply_tile(2 * pair - 1, y_bank)
-                unpack_bank(pair - 1, y_bank)
+                multiply_tile(2 * pair, y_bank)
+                multiply_tile(2 * pair + 1, y_bank)
+                unpack_bank(pair, y_bank)
         hold_clock(BURST)
 
         lam_bank = banks.tile([P, 4 * D], F32, tag="bank", name="lam_bank")
@@ -240,11 +239,22 @@ def tile_differentialattention_pa_s_kernel(tc, x, Wq, Wk, lq1, lq2, lk1, lk2, ou
         sums = keep.tile([P, QUAD], F32, name="sums")
         inverse = keep.tile([P, QUAD], F32, name="inverse")
         for chunk in range(CHUNKS + 1):
+            ts = slice(chunk * CHUNK, (chunk + 1) * CHUNK)
+            done = slice((chunk - 1) * CHUNK, chunk * CHUNK)
+            if chunk >= 1:
+                nc.vector.tensor_reduce(
+                    out=sums[:, done],
+                    in_=expd[:, :, done].rearrange("p m t -> p t m"),
+                    axis=AXIS.X,
+                    op=ALU.add,
+                )
             if chunk < CHUNKS:
-                ts = slice(chunk * CHUNK, (chunk + 1) * CHUNK)
                 nc.vector.tensor_reduce(
                     out=top[:, ts], in_=scores[chunk][:, :, 0:ROWS], axis=AXIS.X, op=ALU.max
                 )
+            if chunk >= 1:
+                nc.vector.reciprocal(out=inverse[:, done], in_=sums[:, done])
+            if chunk < CHUNKS:
                 nc.vector.tensor_tensor(
                     out=expd[:, :, ts],
                     in0=scores[chunk][:, :, 0:ROWS].rearrange("p t m -> p m t"),
@@ -255,18 +265,10 @@ def tile_differentialattention_pa_s_kernel(tc, x, Wq, Wk, lq1, lq2, lk1, lk2, ou
                     out=expd[:, :, ts], in_=expd[:, :, ts], func=ACT.Exp, scale=SCALE
                 )
             if chunk >= 1:
-                ts = slice((chunk - 1) * CHUNK, chunk * CHUNK)
-                nc.vector.tensor_reduce(
-                    out=sums[:, ts],
-                    in_=expd[:, :, ts].rearrange("p m t -> p t m"),
-                    axis=AXIS.X,
-                    op=ALU.add,
-                )
-                nc.vector.reciprocal(out=inverse[:, ts], in_=sums[:, ts])
                 nc.vector.tensor_tensor(
-                    out=expd[:, :, ts],
-                    in0=expd[:, :, ts],
-                    in1=inverse[:, ts].unsqueeze(1).to_broadcast([P, ROWS, CHUNK]),
+                    out=expd[:, :, done],
+                    in0=expd[:, :, done],
+                    in1=inverse[:, done].unsqueeze(1).to_broadcast([P, ROWS, CHUNK]),
                     op=ALU.mult,
                 )
 

@@ -32,8 +32,8 @@ CHUNK = 8
 CHUNKS = QUAD // CHUNK
 SCALE = D ** -0.5
 LAM_INIT = 0.8 - 0.6 * math.exp(-0.3 * 12)
-BURST = 16
-SCORE_COLS = 44
+BURST = 20
+SCORE_COLS = 46
 
 FLOPS = 2 * P * K * 2 * K + 2 * P * ROWS * ROWS * D
 

from contextlib import ExitStack
import math

import concourse.mybir as mybir
from concourse.masks import make_identity

F32 = mybir.dt.float32
BF16 = mybir.dt.bfloat16
U32 = mybir.dt.uint32
U8 = mybir.dt.uint8
I32 = mybir.dt.int32
FP8X4 = mybir.dt.float8_e4m3fn_x4
ALU = mybir.AluOpType
ACT = mybir.ActivationFunctionType
AXIS = mybir.AxisListType

P = 128
K = 1024
K_PASS = 512
PASSES = K // K_PASS
WORDS = K // 2
HEADS = 16
ROWS = 2 * HEADS
D = 32
QUAD = 32
QUADS = P // QUAD
BANK = 512
W_TILES = 4
PAIRS = 4
PAIR_HEADS = 8
CHUNK = 8
CHUNKS = QUAD // CHUNK
SCALE = D ** -0.5
LAM_INIT = 0.8 - 0.6 * math.exp(-0.3 * 12)
BURST = 20
SCORE_COLS = 46

FLOPS = 2 * P * K * 2 * K + 2 * P * ROWS * ROWS * D


def regroup_rows(nc, banks, ident, row_words, grouped_words):
    bank = banks.tile([P, 2 * PASSES, P], F32, tag="bank", name="bank")
    for chunk in range(2 * PASSES):
        nc.tensor.transpose(bank[:, chunk, :], row_words[:, chunk * P : (chunk + 1) * P], ident)
    nc.scalar.copy(
        out=grouped_words.rearrange("p (g r u) -> p g r u", g=PASSES, u=2),
        in_=bank[:].rearrange("p (g u) r -> p g r u", u=2),
    )


def tile_differentialattention_pa_s_kernel(tc, x, Wq, Wk, lq1, lq2, lk1, lk2, out):
    nc = tc.nc
    with ExitStack() as ctx:
        keep = ctx.enter_context(tc.tile_pool(name="keep", bufs=1))
        stage = ctx.enter_context(tc.tile_pool(name="stage", bufs=4))
        banks = ctx.enter_context(tc.psum_pool(name="banks", bufs=5))
        y_pool = ctx.enter_context(tc.psum_pool(name="y_pool", bufs=2))
        idle_pool = ctx.enter_context(tc.psum_pool(name="idle_pool", bufs=1))
        ctx.enter_context(tc.manual_schedule())

        x_sb = keep.tile([P, K], BF16, name="x_sb")
        nc.sync.dma_start(out=x_sb[:], in_=x.rearrange("b n k -> (b n) k"))
        w_tiles = []
        for w in (Wq, Wk):
            w_view = w.rearrange("(s p j) k -> s p (j k)", p=P, j=2)
            for s in range(W_TILES):
                w_sb = keep.tile([P, 2 * K], BF16, name="w_sb%d" % len(w_tiles))
                nc.sync.dma_start(out=w_sb[:], in_=w_view[s])
                w_tiles.append(w_sb)

        lam_rows = keep.tile([P, 4 * D], BF16, name="lam_rows")
        nc.vector.memset(lam_rows[:], 0.0)
        for n, vector in enumerate((lq1, lq2, lk1, lk2)):
            nc.scalar.dma_start(
                out=lam_rows[0:1, n * D : (n + 1) * D], in_=vector.rearrange("(o d) -> o d", o=1)
            )

        ident = keep.tile([P, P], F32, name="ident")
        make_identity(nc, ident[:])
        ones = keep.tile([P, P], BF16, name="ones")
        nc.vector.memset(ones[:], 1.0)
        warm = keep.tile([P, 2], F32, name="warm")
        nc.vector.memset(warm[:], 0.0)
        nc.scalar.activation(out=warm[:, 1:2], in_=warm[:, 0:1], func=ACT.Exp)
        idle_zeros = keep.tile([P, 4 * P], BF16, align_bytes=64, name="idle_zeros")
        idle_codes = keep.tile([P, P], U32, align_bytes=64, name="idle_codes")
        idle_scales = keep.tile([P, P], U8, align_bytes=64, name="idle_scales")
        nc.vector.memset(idle_zeros[:].bitcast(I32), 0)
        nc.vector.quantize_mx(
            out=idle_codes[:].bitcast(FP8X4), scales=idle_scales[:], in_=idle_zeros[:]
        )
        idle_bank = idle_pool.tile([P, P], F32, name="idle_bank")

        def hold_clock(passes):
            for repeat in range(passes):
                nc.tensor.matmul_mx(
                    out=idle_bank[:],
                    lhsT=idle_codes[:].bitcast(FP8X4),
                    lhsT_scale=idle_scales[:],
                    rhs=idle_codes[:].bitcast(FP8X4),
                    rhs_scale=idle_scales[:],
                    start=True,
                    stop=True,
                )

        q_blocks = keep.tile([P, QUAD, QUADS, ROWS], F32, name="q_blocks")
        nc.vector.memset(q_blocks[:], 0.0)
        k_cols = keep.tile([P, QUAD + 1, ROWS], F32, name="k_cols")
        nc.vector.memset(k_cols[:, QUAD, :], 0.0)

        x_grouped = keep.tile([P, PASSES * P * 4], BF16, align_bytes=64, name="x_grouped")
        regroup_rows(nc, banks, ident[:], x_sb[:].bitcast(F32), x_grouped[:].bitcast(F32))
        x_codes = keep.tile([P, PASSES * P], U32, align_bytes=64, name="x_codes")
        x_scales = keep.tile([P, PASSES * P], U8, align_bytes=64, name="x_scales")
        nc.vector.quantize_mx(out=x_codes[:].bitcast(FP8X4), scales=x_scales[:], in_=x_grouped[:])

        grouped = {}
        w_codes = {}
        w_scales = {}

        def regroup_tile(n):
            grouped[n] = stage.tile([P, 2 * PASSES * P * 4], BF16, align_bytes=64, name="grouped")
            for j in range(2):
                words = slice(j * WORDS, (j + 1) * WORDS)
                regroup_rows(
                    nc,
                    banks,
                    ident[:],
                    w_tiles[n][:].bitcast(F32)[:, words],
                    grouped[n][:].bitcast(F32)[:, words],
                )

        def quantise_tile(n):
            w_codes[n] = stage.tile([P, 2 * PASSES * P], U32, align_bytes=64, name="w_codes")
            w_scales[n] = stage.tile([P, 2 * PASSES * P], U8, align_bytes=64, name="w_scales")
            nc.vector.quantize_mx(
                out=w_codes[n][:].bitcast(FP8X4), scales=w_scales[n][:], in_=grouped[n][:]
            )

        def multiply_tile(n, y_bank):
            for j in range(2):
                y_start = j * (BANK // 2) + (n % 2) * P
                for g in range(PASSES):
                    x_cols = slice(g * P, (g + 1) * P)
                    w_cols = slice((j * PASSES + g) * P, (j * PASSES + g + 1) * P)
                    nc.tensor.matmul_mx(
                        out=y_bank[:, y_start : y_start + P],
                        lhsT=x_codes[:, x_cols].bitcast(FP8X4),
                        lhsT_scale=x_scales[:, x_cols],
                        rhs=w_codes[n][:, w_cols].bitcast(FP8X4),
                        rhs_scale=w_scales[n][:, w_cols],
                        start=(g == 0),
                        stop=(g == PASSES - 1),
                    )

        def unpack_bank(pair, y_bank):
            swapped = stage.tile([P, BANK], F32, align_bytes=64, name="swapped")
            nc.vector.transpose(out=swapped[:], in_=y_bank[:])
            heads = slice((pair % 2) * PAIR_HEADS, (pair % 2 + 1) * PAIR_HEADS)
            if pair < PAIRS // 2:
                for c in range(QUADS):
                    rows = slice(c * QUAD, (c + 1) * QUAD)
                    source = swapped[rows, :].rearrange("p (j h t) -> p t j h", j=2, t=QUAD)
                    target = q_blocks[rows, :, c, :].rearrange("p t (j h) -> p t j h", j=2)
                    if c % 2 == 0:
                        nc.vector.tensor_copy(out=target[:, :, :, heads], in_=source)
                    else:
                        nc.gpsimd.tensor_scalar(
                            out=target[:, :, :, heads],
                            in0=source,
                            scalar1=1.0,
                            scalar2=0.0,
                            op0=ALU.mult,
                            op1=ALU.add,
                        )
            else:
                source = swapped[:].rearrange("p (j h t) -> p t j h", j=2, t=QUAD)
                target = k_cols[:, 0:QUAD, :].rearrange("p t (j h) -> p t j h", j=2)
                first = slice(0, QUAD // 2)
                second = slice(QUAD // 2, QUAD)
                nc.vector.tensor_copy(out=target[:, first, :, heads], in_=source[:, first])
                nc.scalar.copy(out=target[:, second, :, heads], in_=source[:, second])

        for weight in range(2):
            tiles = range(weight * W_TILES, (weight + 1) * W_TILES)
            for n in tiles:
                regroup_tile(n)
                if n > tiles[0]:
                    quantise_tile(n - 1)
            quantise_tile(tiles[-1])
            for pair in (2 * weight, 2 * weight + 1):
                y_bank = y_pool.tile([P, BANK], F32, tag="y_bank", name="y_bank")
                multiply_tile(2 * pair, y_bank)
                multiply_tile(2 * pair + 1, y_bank)
                unpack_bank(pair, y_bank)
        hold_clock(BURST)

        lam_bank = banks.tile([P, 4 * D], F32, tag="bank", name="lam_bank")
        nc.tensor.matmul(out=lam_bank[:], lhsT=ones[:], rhs=lam_rows[:], start=True, stop=True)
        lam_all = keep.tile([P, 4 * D], F32, name="lam_all")
        nc.scalar.copy(out=lam_all[:], in_=lam_bank[:])
        lam_prod = keep.tile([P, 2, D], F32, name="lam_prod")
        nc.vector.tensor_tensor(
            out=lam_prod[:].rearrange("p n d -> p (n d)"),
            in0=lam_all[:, 0 : 2 * D],
            in1=lam_all[:, 2 * D : 4 * D],
            op=ALU.mult,
        )
        lam_dots = keep.tile([P, 2], F32, name="lam_dots")
        nc.vector.tensor_reduce(out=lam_dots[:], in_=lam_prod[:], axis=AXIS.X, op=ALU.add)
        lam_exp = keep.tile([P, 2], F32, name="lam_exp")
        nc.scalar.activation(out=lam_exp[:], in_=lam_dots[:], func=ACT.Exp)
        neg_lam = keep.tile([P, 1], F32, name="neg_lam")
        nc.vector.scalar_tensor_tensor(
            out=neg_lam[:],
            in0=lam_exp[:, 1:2],
            scalar=-LAM_INIT,
            in1=lam_exp[:, 0:1],
            op0=ALU.add,
            op1=ALU.subtract,
        )

        k_flat = k_cols[:].rearrange("p t m -> p (t m)")
        scores = []
        for chunk in range(CHUNKS):
            scores.append(banks.tile([P, CHUNK, SCORE_COLS], F32, tag="bank", name="scores"))
            for t in range(CHUNK):
                first_col = (chunk * CHUNK + t) * ROWS
                nc.tensor.matmul(
                    out=scores[chunk][:, t, :],
                    lhsT=q_blocks[:, chunk * CHUNK + t].rearrange("p c i -> p (c i)"),
                    rhs=k_flat[:, first_col : first_col + SCORE_COLS],
                    start=True,
                    stop=True,
                )

        top = keep.tile([P, QUAD], F32, name="top")
        expd = keep.tile([P, ROWS, QUAD], F32, align_bytes=64, name="expd")
        sums = keep.tile([P, QUAD], F32, name="sums")
        inverse = keep.tile([P, QUAD], F32, name="inverse")
        for chunk in range(CHUNKS + 1):
            ts = slice(chunk * CHUNK, (chunk + 1) * CHUNK)
            done = slice((chunk - 1) * CHUNK, chunk * CHUNK)
            if chunk >= 1:
                nc.vector.tensor_reduce(
                    out=sums[:, done],
                    in_=expd[:, :, done].rearrange("p m t -> p t m"),
                    axis=AXIS.X,
                    op=ALU.add,
                )
            if chunk < CHUNKS:
                nc.vector.tensor_reduce(
                    out=top[:, ts], in_=scores[chunk][:, :, 0:ROWS], axis=AXIS.X, op=ALU.max
                )
            if chunk >= 1:
                nc.vector.reciprocal(out=inverse[:, done], in_=sums[:, done])
            if chunk < CHUNKS:
                nc.vector.tensor_tensor(
                    out=expd[:, :, ts],
                    in0=scores[chunk][:, :, 0:ROWS].rearrange("p t m -> p m t"),
                    in1=top[:, ts].unsqueeze(1).to_broadcast([P, ROWS, CHUNK]),
                    op=ALU.subtract,
                )
                nc.scalar.activation(
                    out=expd[:, :, ts], in_=expd[:, :, ts], func=ACT.Exp, scale=SCALE
                )
            if chunk >= 1:
                nc.vector.tensor_tensor(
                    out=expd[:, :, done],
                    in0=expd[:, :, done],
                    in1=inverse[:, done].unsqueeze(1).to_broadcast([P, ROWS, CHUNK]),
                    op=ALU.mult,
                )

        att = keep.tile([P, ROWS * ROWS], F32, align_bytes=64, name="att")
        nc.vector.transpose(out=att[:], in_=expd[:].rearrange("p m t -> p (m t)"))

        att_view = att[:].rearrange("p (m i) -> p i m", i=ROWS)
        result = keep.tile([P, HEADS, HEADS], F32, name="result")
        nc.vector.scalar_tensor_tensor(
            out=result[:],
            in0=att_view[:, HEADS:ROWS, HEADS:ROWS],
            scalar=neg_lam[:, 0:1],
            in1=att_view[:, 0:HEADS, 0:HEADS],
            op0=ALU.mult,
            op1=ALU.add,
        )
        nc.sync.dma_start(
            out=out.rearrange("b n a h -> (b n) (a h)"), in_=result[:].rearrange("p a h -> p (a h)")
        )
